import numpy as np
import ml_dtypes


def mxq(x, axis, fmt="e4m3"):
    dtype, down = {"e4m3": (ml_dtypes.float8_e4m3fn, 7), "e5m2": (ml_dtypes.float8_e5m2, 14)}[fmt]
    v = np.moveaxis(np.asarray(x, np.float32).astype(ml_dtypes.bfloat16).astype(np.float64), axis, -1)
    blocks = v.reshape(v.shape[:-1] + (-1, 32))
    amax = np.abs(blocks).max(-1, keepdims=True)
    byte = np.maximum(np.where(amax > 0, np.frexp(amax)[1] - 1 + 127, 0) - down, 1)
    scale = np.exp2(byte - 127.0)
    codes = (blocks / scale).astype(np.float32).astype(dtype).astype(np.float64)
    return np.moveaxis((codes * scale).reshape(v.shape), -1, axis)


WIDE = False


def mx_kscale(k):
    if not WIDE:
        return np.ones(k)
    levels = np.array([10, -10, 5, -5, 0])
    a = np.random.permutation(np.resize(levels, k // 512 * 4)).reshape(k // 512, 4)
    idx = np.arange(k)
    return np.exp2(a[idx // 512, idx % 128 // 32])


BF16 = ml_dtypes.bfloat16


def bf(x):
    return np.asarray(x, np.float32).astype(BF16)


def f64(x):
    return np.asarray(x).astype(np.float64)


E2M1 = np.array([0.0, 0.5, 1.0, 1.5, 2.0, 3.0, 4.0, 6.0, -0.0, -0.5, -1.0, -1.5, -2.0, -3.0, -4.0, -6.0])


def pack_weight(w, fmt):
    k, n = w.shape
    w = f64(bf(w)).reshape(k // 32, 32, n)
    amax = np.abs(w).max(1)
    if fmt == "e4m3":
        byte = np.frexp(amax)[1] - 1 + 127 - 7
    else:
        mant, ex = np.frexp(amax / 6.0)
        byte = np.where(mant > 0.5, ex, ex - 1) + 127
    byte = np.clip(np.where(amax > 0, byte, 1), 1, 254)
    scaled = (w * np.exp2(127.0 - byte)[:, None, :]).reshape(k, n).astype(np.float32)
    by_word = np.ascontiguousarray(scaled.reshape(k // 512, 128, 4, n).transpose(0, 1, 3, 2))
    if fmt == "e4m3":
        words = by_word.astype(ml_dtypes.float8_e4m3fn).view(np.uint8)
    else:
        c = by_word.astype(ml_dtypes.float4_e2m1fn).view(np.uint8) & 0xF
        words = c[..., 0::2] | (c[..., 1::2] << 4)
    return np.ascontiguousarray(words), np.ascontiguousarray(byte.astype(np.uint8).reshape(k // 512, 16, n))


def unpack_weight(words, scales, fmt):
    g, p, n, _ = words.shape
    if fmt == "e4m3":
        vals = np.ascontiguousarray(words).view(ml_dtypes.float8_e4m3fn).astype(np.float64)
    else:
        nib = np.empty((g, p, n, 4), np.uint8)
        nib[..., 0::2] = words & 0xF
        nib[..., 1::2] = words >> 4
        vals = E2M1[nib]
    vals = vals * np.repeat(np.exp2(scales.astype(np.float64) - 127.0), 8, axis=1)[..., None]
    return vals.transpose(0, 1, 3, 2).reshape(g * 512, n)


B, T, G, I, H = 4, 1024, 4, 512, 128
FMT = "e4m3"


def setup_inputs():
    s = mx_kscale(I)
    x = bf((np.random.standard_normal((B, T, G, I)) * s).reshape(B, T, G * I))
    w = np.random.standard_normal((G, H, I)) / np.sqrt(I) / s
    stack = np.swapaxes(w, 1, 2)
    words, scales = pack_weight(stack.reshape(-1, H), FMT)
    b = bf(np.random.standard_normal((G, H)) * 0.5)
    return {"x": x, "W_words": words, "W_scales": scales, "b": b}


def reference(x, W_words, W_scales, b):
    xg = f64(x).reshape(B, T, G, I)
    xq = mxq(xg, 3, "e4m3")
    wq = unpack_weight(W_words, W_scales, FMT).reshape(G, I, H)
    y = xq.transpose(2, 0, 1, 3).reshape(G, B * T, I) @ wq
    out = y.reshape(G, B, T, H).transpose(1, 2, 0, 3) + f64(b)
    return np.swapaxes(out, -1, -2).reshape(B, T, G * H)

@@ -1,0 +1,149 @@
+from contextlib import ExitStack
+
+import concourse.mybir as mybir
+from concourse.masks import make_identity
+
+BF16 = mybir.dt.bfloat16
+F32 = mybir.dt.float32
+I32 = mybir.dt.int32
+U32 = mybir.dt.uint32
+U8 = mybir.dt.uint8
+FP8X4 = mybir.dt.float8_e4m3fn_x4
+
+P = 128
+PACK = 4
+GROUPS = 4
+K_GROUP = P * PACK
+H = 128
+FEATURES = GROUPS * K_GROUP
+CHANNELS = GROUPS * H
+TOKENS = 4 * 1024
+TILES = TOKENS // P
+WORDS_GROUP = K_GROUP // 2
+BANK_GROUPS = 2
+
+TILES_PER_ROUND = 2
+ROUNDS = TILES // TILES_PER_ROUND
+
+FLOPS = 2 * TOKENS * GROUPS * K_GROUP * H
+
+
+def tile_groupedlinear_t_e_kernel(tc, x, W_words, W_scales, b, out):
+    nc = tc.nc
+    x_rows = x.flatten_outer_dims().rearrange("(p j) f -> p j f", j=TILES)
+    out_rows = out.flatten_outer_dims().rearrange("(p j) c -> p j c", j=TILES)
+
+    with ExitStack() as ctx:
+        consts = ctx.enter_context(tc.tile_pool(name="consts", bufs=1))
+        resident = ctx.enter_context(tc.tile_pool(name="resident", bufs=1))
+        stage = ctx.enter_context(tc.tile_pool(name="stage", bufs=2 * TILES_PER_ROUND))
+        xt_pool = ctx.enter_context(tc.psum_pool(name="xt_pool", bufs=6))
+        acc_pool = ctx.enter_context(tc.psum_pool(name="acc_pool", bufs=TILES_PER_ROUND))
+        ctx.enter_context(tc.manual_schedule())
+
+        x_sb = []
+        out_sb = []
+        for r in range(ROUNDS):
+            x_sb.append(resident.tile([P, TILES_PER_ROUND, FEATURES], BF16, name="x%d" % r))
+            out_sb.append(resident.tile([P, TILES_PER_ROUND, CHANNELS], F32, name="out%d" % r))
+
+        ident = consts.tile([P, P], F32)
+        w_codes = consts.tile([P, GROUPS, H], U32, align_bytes=64)
+        w_scales = consts.tile([P, GROUPS, H], U8, align_bytes=64)
+        bias_rows = consts.tile([P, CHANNELS], BF16)
+        ones = consts.tile([P, P], BF16)
+        bias_sb = consts.tile([P, H, GROUPS], F32)
+
+        make_identity(nc, ident[:])
+        nc.vector.memset(w_scales[:].bitcast(I32), 0)
+        nc.vector.memset(bias_rows[:], 0.0)
+        nc.vector.memset(ones[:], 1.0)
+
+        def load_round(r):
+            tiles = slice(r * TILES_PER_ROUND, (r + 1) * TILES_PER_ROUND)
+            nc.sync.dma_start(out=x_sb[r][:], in_=x_rows[:, tiles, :])
+
+        for i in range(TILES_PER_ROUND):
+            nc.sync.dma_start(out=x_sb[0][:, i, :], in_=x_rows[:, i, :])
+        load_round(1)
+        nc.sync.dma_start(
+            out=w_codes[:].bitcast(I32),
+            in_=W_words.rearrange("g p n t -> p g (n t)").bitcast(I32),
+        )
+        scale_rows = W_scales.rearrange("g (Q r) n -> r Q g n", r=4)
+        for r in range(4):
+            nc.sync.dma_start(out=w_scales[r:P:32, :, :].bitcast(I32), in_=scale_rows[r].bitcast(I32))
+        nc.sync.dma_start(out=bias_rows[0:1, :], in_=b.rearrange("g h -> (g h)").unsqueeze(0))
+        for r in range(2, ROUNDS):
+            load_round(r)
+
+        def transpose_and_quantise(r):
+            quantised = []
+            for i in range(TILES_PER_ROUND):
+                x_words = x_sb[r][:, i, :].bitcast(F32)
+                grouped = stage.tile([P, GROUPS * P * PACK], BF16, align_bytes=64)
+                grouped_words = grouped[:].bitcast(F32)
+                for bank in range(GROUPS // BANK_GROUPS):
+                    xt = xt_pool.tile([P, 2, BANK_GROUPS * P], F32)
+                    for g2 in range(BANK_GROUPS):
+                        first = (bank * BANK_GROUPS + g2) * WORDS_GROUP
+                        for u in range(2):
+                            nc.tensor.transpose(
+                                xt[:, u, g2 * P : (g2 + 1) * P],
+                                x_words[:, first + u : first + WORDS_GROUP : 2],
+                                ident[:],
+                            )
+                    bank_words = slice(bank * 2 * BANK_GROUPS * P, (bank + 1) * 2 * BANK_GROUPS * P)
+                    nc.scalar.copy(
+                        out=grouped_words[:, bank_words].rearrange("p (c u) -> p c u", u=2),
+                        in_=xt[:].rearrange("p u c -> p c u"),
+                    )
+                x_codes = stage.tile([P, GROUPS * P], U32, align_bytes=64)
+                x_scales = stage.tile([P, GROUPS * P], U8, align_bytes=64)
+                nc.vector.quantize_mx(out=x_codes[:].bitcast(FP8X4), scales=x_scales[:], in_=grouped[:])
+                quantised.append((x_codes, x_scales))
+            return quantised
+
+        def multiply_and_store(r, quantised):
+            for i in range(TILES_PER_ROUND):
+                x_codes, x_scales = quantised[i]
+                acc = acc_pool.tile([P, GROUPS, H], F32, tag="acc")
+                for g in range(GROUPS):
+                    tokens = slice(g * P, (g + 1) * P)
+                    nc.tensor.matmul_mx(
+                        out=acc[:, g, :],
+                        lhsT=x_codes[:, tokens].bitcast(FP8X4),
+                        lhsT_scale=x_scales[:, tokens],
+                        rhs=w_codes[:, g, :].bitcast(FP8X4),
+                        rhs_scale=w_scales[:, g, :],
+                        start=True,
+                        stop=True,
+                    )
+                nc.vector.tensor_tensor(
+                    out=out_sb[r][:, i, :].rearrange("p (h g) -> p h g", g=GROUPS),
+                    in0=acc[:].rearrange("p g h -> p h g"),
+                    in1=bias_sb[:],
+                    op=mybir.AluOpType.add,
+                )
+            tiles = slice(r * TILES_PER_ROUND, (r + 1) * TILES_PER_ROUND)
+            nc.sync.dma_start(out=out_rows[:, tiles, :], in_=out_sb[r][:])
+
+        def spread_bias():
+            bias_ps = acc_pool.tile([P, GROUPS, H], F32, tag="acc")
+            nc.tensor.matmul(
+                out=bias_ps[:].rearrange("p g h -> p (g h)"),
+                lhsT=ones[:],
+                rhs=bias_rows[:],
+                start=True,
+                stop=True,
+            )
+            nc.vector.tensor_copy(out=bias_sb[:], in_=bias_ps[:].rearrange("p g h -> p h g"))
+
+        waiting = transpose_and_quantise(0)
+        for r in range(1, ROUNDS):
+            fresh = transpose_and_quantise(r)
+            if r == 1:
+                spread_bias()
+            multiply_and_store(r - 1, waiting)
+            waiting = fresh
+        multiply_and_store(ROUNDS - 1, waiting)

@@ -25,6 +25,10 @@ BANK_GROUPS = 2
 TILES_PER_ROUND = 2
 ROUNDS = TILES // TILES_PER_ROUND
 
+HEAD_TILES = 4 * TILES_PER_ROUND
+LOAD_TILES = 4
+STORE_TILES = 4
+
 FLOPS = 2 * TOKENS * GROUPS * K_GROUP * H
 
 
@@ -41,11 +45,14 @@ def tile_groupedlinear_t_e_kernel(tc, x, W_words, W_scales, b, out):
         acc_pool = ctx.enter_context(tc.psum_pool(name="acc_pool", bufs=TILES_PER_ROUND))
         ctx.enter_context(tc.manual_schedule())
 
-        x_sb = []
-        out_sb = []
-        for r in range(ROUNDS):
-            x_sb.append(resident.tile([P, TILES_PER_ROUND, FEATURES], BF16, name="x%d" % r))
-            out_sb.append(resident.tile([P, TILES_PER_ROUND, CHANNELS], F32, name="out%d" % r))
+        x_tiles = []
+        out_tiles = []
+        out_chunks = []
+        for first in range(0, TILES, STORE_TILES):
+            chunk = resident.tile([P, STORE_TILES, CHANNELS], F32, name="out%d" % first)
+            out_chunks.append(chunk)
+            for i in range(STORE_TILES):
+                out_tiles.append(chunk[:, i, :])
 
         ident = consts.tile([P, P], F32)
         w_codes = consts.tile([P, GROUPS, H], U32, align_bytes=64)
@@ -59,13 +66,14 @@ def tile_groupedlinear_t_e_kernel(tc, x, W_words, W_scales, b, out):
         nc.vector.memset(bias_rows[:], 0.0)
         nc.vector.memset(ones[:], 1.0)
 
-        def load_round(r):
-            tiles = slice(r * TILES_PER_ROUND, (r + 1) * TILES_PER_ROUND)
-            nc.sync.dma_start(out=x_sb[r][:], in_=x_rows[:, tiles, :])
+        def load_tiles(first, count):
+            chunk = resident.tile([P, count, FEATURES], BF16, name="x%d" % first)
+            nc.sync.dma_start(out=chunk[:], in_=x_rows[:, first : first + count, :])
+            for i in range(count):
+                x_tiles.append(chunk[:, i, :])
 
-        for i in range(TILES_PER_ROUND):
-            nc.sync.dma_start(out=x_sb[0][:, i, :], in_=x_rows[:, i, :])
-        load_round(1)
+        for j in range(2 * TILES_PER_ROUND):
+            load_tiles(j, 1)
         nc.sync.dma_start(
             out=w_codes[:].bitcast(I32),
             in_=W_words.rearrange("g p n t -> p g (n t)").bitcast(I32),
@@ -74,13 +82,15 @@ def tile_groupedlinear_t_e_kernel(tc, x, W_words, W_scales, b, out):
         for r in range(4):
             nc.sync.dma_start(out=w_scales[r:P:32, :, :].bitcast(I32), in_=scale_rows[r].bitcast(I32))
         nc.sync.dma_start(out=bias_rows[0:1, :], in_=b.rearrange("g h -> (g h)").unsqueeze(0))
-        for r in range(2, ROUNDS):
-            load_round(r)
+        for j in range(2 * TILES_PER_ROUND, HEAD_TILES):
+            load_tiles(j, 1)
+        for j in range(HEAD_TILES, TILES, LOAD_TILES):
+            load_tiles(j, LOAD_TILES)
 
         def transpose_and_quantise(r):
             quantised = []
-            for i in range(TILES_PER_ROUND):
-                x_words = x_sb[r][:, i, :].bitcast(F32)
+            for j in range(r * TILES_PER_ROUND, (r + 1) * TILES_PER_ROUND):
+                x_words = x_tiles[j].bitcast(F32)
                 grouped = stage.tile([P, GROUPS * P * PACK], BF16, align_bytes=64)
                 grouped_words = grouped[:].bitcast(F32)
                 for bank in range(GROUPS // BANK_GROUPS):
@@ -106,6 +116,7 @@ def tile_groupedlinear_t_e_kernel(tc, x, W_words, W_scales, b, out):
 
         def multiply_and_store(r, quantised):
             for i in range(TILES_PER_ROUND):
+                j = r * TILES_PER_ROUND + i
                 x_codes, x_scales = quantised[i]
                 acc = acc_pool.tile([P, GROUPS, H], F32, tag="acc")
                 for g in range(GROUPS):
@@ -120,13 +131,14 @@ def tile_groupedlinear_t_e_kernel(tc, x, W_words, W_scales, b, out):
                         stop=True,
                     )
                 nc.vector.tensor_tensor(
-                    out=out_sb[r][:, i, :].rearrange("p (h g) -> p h g", g=GROUPS),
+                    out=out_tiles[j].rearrange("p (h g) -> p h g", g=GROUPS),
                     in0=acc[:].rearrange("p g h -> p h g"),
                     in1=bias_sb[:],
                     op=mybir.AluOpType.add,
                 )
-            tiles = slice(r * TILES_PER_ROUND, (r + 1) * TILES_PER_ROUND)
-            nc.sync.dma_start(out=out_rows[:, tiles, :], in_=out_sb[r][:])
+                if (j + 1) % STORE_TILES == 0:
+                    tiles = slice(j + 1 - STORE_TILES, j + 1)
+                    nc.sync.dma_start(out=out_rows[:, tiles, :], in_=out_chunks[j // STORE_TILES][:])
 
         def spread_bias():
             bias_ps = acc_pool.tile([P, GROUPS, H], F32, tag="acc")

@@ -24,10 +24,7 @@ BANK_GROUPS = 2
 
 TILES_PER_ROUND = 2
 ROUNDS = TILES // TILES_PER_ROUND
-
-HEAD_TILES = 4 * TILES_PER_ROUND
-LOAD_TILES = 4
-STORE_TILES = 4
+HEAD_ROUNDS = 4
 
 FLOPS = 2 * TOKENS * GROUPS * K_GROUP * H
 
@@ -45,14 +42,11 @@ def tile_groupedlinear_t_e_kernel(tc, x, W_words, W_scales, b, out):
         acc_pool = ctx.enter_context(tc.psum_pool(name="acc_pool", bufs=TILES_PER_ROUND))
         ctx.enter_context(tc.manual_schedule())
 
-        x_tiles = []
-        out_tiles = []
-        out_chunks = []
-        for first in range(0, TILES, STORE_TILES):
-            chunk = resident.tile([P, STORE_TILES, CHANNELS], F32, name="out%d" % first)
-            out_chunks.append(chunk)
-            for i in range(STORE_TILES):
-                out_tiles.append(chunk[:, i, :])
+        x_sb = []
+        out_sb = []
+        for r in range(ROUNDS):
+            x_sb.append(resident.tile([P, TILES_PER_ROUND, FEATURES], BF16, name="x%d" % r))
+            out_sb.append(resident.tile([P, TILES_PER_ROUND, CHANNELS], F32, name="out%d" % r))
 
         ident = consts.tile([P, P], F32)
         w_codes = consts.tile([P, GROUPS, H], U32, align_bytes=64)
@@ -66,14 +60,16 @@ def tile_groupedlinear_t_e_kernel(tc, x, W_words, W_scales, b, out):
         nc.vector.memset(bias_rows[:], 0.0)
         nc.vector.memset(ones[:], 1.0)
 
-        def load_tiles(first, count):
-            chunk = resident.tile([P, count, FEATURES], BF16, name="x%d" % first)
-            nc.sync.dma_start(out=chunk[:], in_=x_rows[:, first : first + count, :])
-            for i in range(count):
-                x_tiles.append(chunk[:, i, :])
+        def load_round(r):
+            first = r * TILES_PER_ROUND
+            if r < HEAD_ROUNDS:
+                for i in range(TILES_PER_ROUND):
+                    nc.sync.dma_start(out=x_sb[r][:, i, :], in_=x_rows[:, first + i, :])
+            else:
+                nc.sync.dma_start(out=x_sb[r][:], in_=x_rows[:, first : first + TILES_PER_ROUND, :])
 
-        for j in range(2 * TILES_PER_ROUND):
-            load_tiles(j, 1)
+        load_round(0)
+        load_round(1)
         nc.sync.dma_start(
             out=w_codes[:].bitcast(I32),
             in_=W_words.rearrange("g p n t -> p g (n t)").bitcast(I32),
@@ -82,15 +78,13 @@ def tile_groupedlinear_t_e_kernel(tc, x, W_words, W_scales, b, out):
         for r in range(4):
             nc.sync.dma_start(out=w_scales[r:P:32, :, :].bitcast(I32), in_=scale_rows[r].bitcast(I32))
         nc.sync.dma_start(out=bias_rows[0:1, :], in_=b.rearrange("g h -> (g h)").unsqueeze(0))
-        for j in range(2 * TILES_PER_ROUND, HEAD_TILES):
-            load_tiles(j, 1)
-        for j in range(HEAD_TILES, TILES, LOAD_TILES):
-            load_tiles(j, LOAD_TILES)
+        for r in range(2, ROUNDS):
+            load_round(r)
 
         def transpose_and_quantise(r):
             quantised = []
-            for j in range(r * TILES_PER_ROUND, (r + 1) * TILES_PER_ROUND):
-                x_words = x_tiles[j].bitcast(F32)
+            for i in range(TILES_PER_ROUND):
+                x_words = x_sb[r][:, i, :].bitcast(F32)
                 grouped = stage.tile([P, GROUPS * P * PACK], BF16, align_bytes=64)
                 grouped_words = grouped[:].bitcast(F32)
                 for bank in range(GROUPS // BANK_GROUPS):
@@ -116,7 +110,6 @@ def tile_groupedlinear_t_e_kernel(tc, x, W_words, W_scales, b, out):
 
         def multiply_and_store(r, quantised):
             for i in range(TILES_PER_ROUND):
-                j = r * TILES_PER_ROUND + i
                 x_codes, x_scales = quantised[i]
                 acc = acc_pool.tile([P, GROUPS, H], F32, tag="acc")
                 for g in range(GROUPS):
@@ -131,14 +124,13 @@ def tile_groupedlinear_t_e_kernel(tc, x, W_words, W_scales, b, out):
                         stop=True,
                     )
                 nc.vector.tensor_tensor(
-                    out=out_tiles[j].rearrange("p (h g) -> p h g", g=GROUPS),
+                    out=out_sb[r][:, i, :].rearrange("p (h g) -> p h g", g=GROUPS),
                     in0=acc[:].rearrange("p g h -> p h g"),
                     in1=bias_sb[:],
                     op=mybir.AluOpType.add,
                 )
-                if (j + 1) % STORE_TILES == 0:
-                    tiles = slice(j + 1 - STORE_TILES, j + 1)
-                    nc.sync.dma_start(out=out_rows[:, tiles, :], in_=out_chunks[j // STORE_TILES][:])
+            tiles = slice(r * TILES_PER_ROUND, (r + 1) * TILES_PER_ROUND)
+            nc.sync.dma_start(out=out_rows[:, tiles, :], in_=out_sb[r][:])
 
         def spread_bias():
             bias_ps = acc_pool.tile([P, GROUPS, H], F32, tag="acc")

@@ -51,14 +51,15 @@ def tile_groupedlinear_t_e_kernel(tc, x, W_words, W_scales, b, out):
         ident = consts.tile([P, P], F32)
         w_codes = consts.tile([P, GROUPS, H], U32, align_bytes=64)
         w_scales = consts.tile([P, GROUPS, H], U8, align_bytes=64)
+        bias_row = consts.tile([1, CHANNELS], BF16)
         bias_rows = consts.tile([P, CHANNELS], BF16)
         ones = consts.tile([P, P], BF16)
         bias_sb = consts.tile([P, H, GROUPS], F32)
 
         make_identity(nc, ident[:])
-        nc.vector.memset(w_scales[:].bitcast(I32), 0)
         nc.vector.memset(bias_rows[:], 0.0)
         nc.vector.memset(ones[:], 1.0)
+        nc.vector.memset(w_scales[:].bitcast(I32), 0)
 
         def load_round(r):
             first = r * TILES_PER_ROUND
@@ -68,6 +69,7 @@ def tile_groupedlinear_t_e_kernel(tc, x, W_words, W_scales, b, out):
             else:
                 nc.sync.dma_start(out=x_sb[r][:], in_=x_rows[:, first : first + TILES_PER_ROUND, :])
 
+        nc.sync.dma_start(out=bias_row[:], in_=b.rearrange("g h -> (g h)").unsqueeze(0))
         load_round(0)
         load_round(1)
         nc.sync.dma_start(
@@ -77,7 +79,6 @@ def tile_groupedlinear_t_e_kernel(tc, x, W_words, W_scales, b, out):
         scale_rows = W_scales.rearrange("g (Q r) n -> r Q g n", r=4)
         for r in range(4):
             nc.sync.dma_start(out=w_scales[r:P:32, :, :].bitcast(I32), in_=scale_rows[r].bitcast(I32))
-        nc.sync.dma_start(out=bias_rows[0:1, :], in_=b.rearrange("g h -> (g h)").unsqueeze(0))
         for r in range(2, ROUNDS):
             load_round(r)
 
@@ -133,6 +134,7 @@ def tile_groupedlinear_t_e_kernel(tc, x, W_words, W_scales, b, out):
             nc.sync.dma_start(out=out_rows[:, tiles, :], in_=out_sb[r][:])
 
         def spread_bias():
+            nc.vector.tensor_copy(out=bias_rows[0:1, :], in_=bias_row[:])
             bias_ps = acc_pool.tile([P, GROUPS, H], F32, tag="acc")
             nc.tensor.matmul(
                 out=bias_ps[:].rearrange("p g h -> p (g h)"),
@@ -143,11 +145,10 @@ def tile_groupedlinear_t_e_kernel(tc, x, W_words, W_scales, b, out):
             )
             nc.vector.tensor_copy(out=bias_sb[:], in_=bias_ps[:].rearrange("p g h -> p h g"))
 
+        spread_bias()
         waiting = transpose_and_quantise(0)
         for r in range(1, ROUNDS):
             fresh = transpose_and_quantise(r)
-            if r == 1:
-                spread_bias()
             multiply_and_store(r - 1, waiting)
             waiting = fresh
         multiply_and_store(ROUNDS - 1, waiting)

@@ -25,6 +25,7 @@ BANK_GROUPS = 2
 TILES_PER_ROUND = 2
 ROUNDS = TILES // TILES_PER_ROUND
 HEAD_ROUNDS = 4
+WARM_UP = 3
 
 FLOPS = 2 * TOKENS * GROUPS * K_GROUP * H
 
@@ -54,16 +55,23 @@ def tile_groupedlinear_t_e_kernel(tc, x, W_words, W_scales, b, out):
         bias_row = consts.tile([1, CHANNELS], BF16)
         bias_rows = consts.tile([P, CHANNELS], BF16)
         ones = consts.tile([P, P], BF16)
+        zeros = consts.tile([P, CHANNELS], BF16)
         bias_sb = consts.tile([P, H, GROUPS], F32)
 
         make_identity(nc, ident[:])
-        nc.vector.memset(bias_rows[:], 0.0)
         nc.vector.memset(ones[:], 1.0)
+        nc.vector.memset(zeros[:], 0.0)
+        nc.vector.memset(bias_rows[:], 0.0)
         nc.vector.memset(w_scales[:].bitcast(I32), 0)
 
         def load_round(r):
             first = r * TILES_PER_ROUND
-            if r < HEAD_ROUNDS:
+            if r == 0:
+                for g in range(GROUPS):
+                    features = slice(g * K_GROUP, (g + 1) * K_GROUP)
+                    nc.sync.dma_start(out=x_sb[0][:, 0, features], in_=x_rows[:, 0, features])
+                nc.sync.dma_start(out=x_sb[0][:, 1, :], in_=x_rows[:, 1, :])
+            elif r < HEAD_ROUNDS:
                 for i in range(TILES_PER_ROUND):
                     nc.sync.dma_start(out=x_sb[r][:, i, :], in_=x_rows[:, first + i, :])
             else:
@@ -89,7 +97,7 @@ def tile_groupedlinear_t_e_kernel(tc, x, W_words, W_scales, b, out):
                 grouped = stage.tile([P, GROUPS * P * PACK], BF16, align_bytes=64)
                 grouped_words = grouped[:].bitcast(F32)
                 for bank in range(GROUPS // BANK_GROUPS):
-                    xt = xt_pool.tile([P, 2, BANK_GROUPS * P], F32)
+                    xt = xt_pool.tile([P, 2, BANK_GROUPS * P], F32, tag="xt")
                     for g2 in range(BANK_GROUPS):
                         first = (bank * BANK_GROUPS + g2) * WORDS_GROUP
                         for u in range(2):
@@ -130,8 +138,11 @@ def tile_groupedlinear_t_e_kernel(tc, x, W_words, W_scales, b, out):
                     in1=bias_sb[:],
                     op=mybir.AluOpType.add,
                 )
-            tiles = slice(r * TILES_PER_ROUND, (r + 1) * TILES_PER_ROUND)
-            nc.sync.dma_start(out=out_rows[:, tiles, :], in_=out_sb[r][:])
+                if r == ROUNDS - 1:
+                    nc.sync.dma_start(out=out_rows[:, r * TILES_PER_ROUND + i, :], in_=out_sb[r][:, i, :])
+            if r < ROUNDS - 1:
+                tiles = slice(r * TILES_PER_ROUND, (r + 1) * TILES_PER_ROUND)
+                nc.sync.dma_start(out=out_rows[:, tiles, :], in_=out_sb[r][:])
 
         def spread_bias():
             nc.vector.tensor_copy(out=bias_rows[0:1, :], in_=bias_row[:])
@@ -145,6 +156,9 @@ def tile_groupedlinear_t_e_kernel(tc, x, W_words, W_scales, b, out):
             )
             nc.vector.tensor_copy(out=bias_sb[:], in_=bias_ps[:].rearrange("p g h -> p h g"))
 
+        warm = xt_pool.tile([P, CHANNELS], F32, tag="xt")
+        for n in range(WARM_UP):
+            nc.tensor.matmul(out=warm[:], lhsT=ones[:], rhs=zeros[:], start=True, stop=True)
         spread_bias()
         waiting = transpose_and_quantise(0)
         for r in range(1, ROUNDS):

@@ -39,8 +39,8 @@ def tile_groupedlinear_t_e_kernel(tc, x, W_words, W_scales, b, out):
         consts = ctx.enter_context(tc.tile_pool(name="consts", bufs=1))
         resident = ctx.enter_context(tc.tile_pool(name="resident", bufs=1))
         stage = ctx.enter_context(tc.tile_pool(name="stage", bufs=2 * TILES_PER_ROUND))
-        xt_pool = ctx.enter_context(tc.psum_pool(name="xt_pool", bufs=6))
-        acc_pool = ctx.enter_context(tc.psum_pool(name="acc_pool", bufs=TILES_PER_ROUND))
+        xt_pool = ctx.enter_context(tc.psum_pool(name="xt_pool", bufs=4))
+        acc_pool = ctx.enter_context(tc.psum_pool(name="acc_pool", bufs=2 * TILES_PER_ROUND))
         ctx.enter_context(tc.manual_schedule())
 
         x_sb = []

@@ -24,8 +24,11 @@ BANK_GROUPS = 2
 
 TILES_PER_ROUND = 2
 ROUNDS = TILES // TILES_PER_ROUND
-HEAD_ROUNDS = 4
+LOAD_TILES = [1, 1, 1, 1, 1, 1, 1, 1, 2, 4, 4, 4, 8, 2]
+W_BEHIND_LOADS = 4
+STORE_TILES = [8, 8, 4, 4, 2, 2, 2, 1, 1]
 WARM_UP = 3
+assert sum(LOAD_TILES) == TILES and sum(STORE_TILES) == TILES
 
 FLOPS = 2 * TOKENS * GROUPS * K_GROUP * H
 
@@ -43,11 +46,8 @@ def tile_groupedlinear_t_e_kernel(tc, x, W_words, W_scales, b, out):
         acc_pool = ctx.enter_context(tc.psum_pool(name="acc_pool", bufs=2 * TILES_PER_ROUND))
         ctx.enter_context(tc.manual_schedule())
 
-        x_sb = []
-        out_sb = []
-        for r in range(ROUNDS):
-            x_sb.append(resident.tile([P, TILES_PER_ROUND, FEATURES], BF16, name="x%d" % r))
-            out_sb.append(resident.tile([P, TILES_PER_ROUND, CHANNELS], F32, name="out%d" % r))
+        x_sb = resident.tile([P, TILES, FEATURES], BF16)
+        out_sb = resident.tile([P, TILES, CHANNELS], F32)
 
         ident = consts.tile([P, P], F32)
         w_codes = consts.tile([P, GROUPS, H], U32, align_bytes=64)
@@ -64,22 +64,14 @@ def tile_groupedlinear_t_e_kernel(tc, x, W_words, W_scales, b, out):
         nc.vector.memset(bias_rows[:], 0.0)
         nc.vector.memset(w_scales[:].bitcast(I32), 0)
 
-        def load_round(r):
-            first = r * TILES_PER_ROUND
-            if r == 0:
-                for g in range(GROUPS):
-                    features = slice(g * K_GROUP, (g + 1) * K_GROUP)
-                    nc.sync.dma_start(out=x_sb[0][:, 0, features], in_=x_rows[:, 0, features])
-                nc.sync.dma_start(out=x_sb[0][:, 1, :], in_=x_rows[:, 1, :])
-            elif r < HEAD_ROUNDS:
-                for i in range(TILES_PER_ROUND):
-                    nc.sync.dma_start(out=x_sb[r][:, i, :], in_=x_rows[:, first + i, :])
-            else:
-                nc.sync.dma_start(out=x_sb[r][:], in_=x_rows[:, first : first + TILES_PER_ROUND, :])
+        def load_tiles(n):
+            first = sum(LOAD_TILES[:n])
+            tiles = slice(first, first + LOAD_TILES[n])
+            nc.sync.dma_start(out=x_sb[:, tiles, :], in_=x_rows[:, tiles, :])
 
         nc.sync.dma_start(out=bias_row[:], in_=b.rearrange("g h -> (g h)").unsqueeze(0))
-        load_round(0)
-        load_round(1)
+        for n in range(W_BEHIND_LOADS):
+            load_tiles(n)
         nc.sync.dma_start(
             out=w_codes[:].bitcast(I32),
             in_=W_words.rearrange("g p n t -> p g (n t)").bitcast(I32),
@@ -87,13 +79,13 @@ def tile_groupedlinear_t_e_kernel(tc, x, W_words, W_scales, b, out):
         scale_rows = W_scales.rearrange("g (Q r) n -> r Q g n", r=4)
         for r in range(4):
             nc.sync.dma_start(out=w_scales[r:P:32, :, :].bitcast(I32), in_=scale_rows[r].bitcast(I32))
-        for r in range(2, ROUNDS):
-            load_round(r)
+        for n in range(W_BEHIND_LOADS, len(LOAD_TILES)):
+            load_tiles(n)
 
         def transpose_and_quantise(r):
             quantised = []
             for i in range(TILES_PER_ROUND):
-                x_words = x_sb[r][:, i, :].bitcast(F32)
+                x_words = x_sb[:, r * TILES_PER_ROUND + i, :].bitcast(F32)
                 grouped = stage.tile([P, GROUPS * P * PACK], BF16, align_bytes=64)
                 grouped_words = grouped[:].bitcast(F32)
                 for bank in range(GROUPS // BANK_GROUPS):
@@ -133,16 +125,16 @@ def tile_groupedlinear_t_e_kernel(tc, x, W_words, W_scales, b, out):
                         stop=True,
                     )
                 nc.vector.tensor_tensor(
-                    out=out_sb[r][:, i, :].rearrange("p (h g) -> p h g", g=GROUPS),
+                    out=out_sb[:, r * TILES_PER_ROUND + i, :].rearrange("p (h g) -> p h g", g=GROUPS),
                     in0=acc[:].rearrange("p g h -> p h g"),
                     in1=bias_sb[:],
                     op=mybir.AluOpType.add,
                 )
-                if r == ROUNDS - 1:
-                    nc.sync.dma_start(out=out_rows[:, r * TILES_PER_ROUND + i, :], in_=out_sb[r][:, i, :])
-            if r < ROUNDS - 1:
-                tiles = slice(r * TILES_PER_ROUND, (r + 1) * TILES_PER_ROUND)
-                nc.sync.dma_start(out=out_rows[:, tiles, :], in_=out_sb[r][:])
+                done = r * TILES_PER_ROUND + i + 1
+                for n in range(len(STORE_TILES)):
+                    if sum(STORE_TILES[: n + 1]) == done:
+                        tiles = slice(done - STORE_TILES[n], done)
+                        nc.sync.dma_start(out=out_rows[:, tiles, :], in_=out_sb[:, tiles, :])
 
         def spread_bias():
             nc.vector.tensor_copy(out=bias_rows[0:1, :], in_=bias_row[:])

from contextlib import ExitStack

import concourse.mybir as mybir
from concourse.masks import make_identity

BF16 = mybir.dt.bfloat16
F32 = mybir.dt.float32
I32 = mybir.dt.int32
U32 = mybir.dt.uint32
U8 = mybir.dt.uint8
FP8X4 = mybir.dt.float8_e4m3fn_x4

P = 128
PACK = 4
GROUPS = 4
K_GROUP = P * PACK
H = 128
FEATURES = GROUPS * K_GROUP
CHANNELS = GROUPS * H
TOKENS = 4 * 1024
TILES = TOKENS // P
WORDS_GROUP = K_GROUP // 2
BANK_GROUPS = 2

TILES_PER_ROUND = 2
ROUNDS = TILES // TILES_PER_ROUND
LOAD_TILES = [1, 1, 1, 1, 1, 1, 1, 1, 2, 4, 4, 4, 8, 2]
W_BEHIND_LOADS = 4
STORE_TILES = [8, 8, 4, 4, 2, 2, 2, 1, 1]
WARM_UP = 3
assert sum(LOAD_TILES) == TILES and sum(STORE_TILES) == TILES

FLOPS = 2 * TOKENS * GROUPS * K_GROUP * H


def tile_groupedlinear_t_e_kernel(tc, x, W_words, W_scales, b, out):
    nc = tc.nc
    x_rows = x.flatten_outer_dims().rearrange("(p j) f -> p j f", j=TILES)
    out_rows = out.flatten_outer_dims().rearrange("(p j) c -> p j c", j=TILES)

    with ExitStack() as ctx:
        consts = ctx.enter_context(tc.tile_pool(name="consts", bufs=1))
        resident = ctx.enter_context(tc.tile_pool(name="resident", bufs=1))
        stage = ctx.enter_context(tc.tile_pool(name="stage", bufs=2 * TILES_PER_ROUND))
        xt_pool = ctx.enter_context(tc.psum_pool(name="xt_pool", bufs=4))
        acc_pool = ctx.enter_context(tc.psum_pool(name="acc_pool", bufs=2 * TILES_PER_ROUND))
        ctx.enter_context(tc.manual_schedule())

        x_sb = resident.tile([P, TILES, FEATURES], BF16)
        out_sb = resident.tile([P, TILES, CHANNELS], F32)

        ident = consts.tile([P, P], F32)
        w_codes = consts.tile([P, GROUPS, H], U32, align_bytes=64)
        w_scales = consts.tile([P, GROUPS, H], U8, align_bytes=64)
        bias_row = consts.tile([1, CHANNELS], BF16)
        bias_rows = consts.tile([P, CHANNELS], BF16)
        ones = consts.tile([P, P], BF16)
        zeros = consts.tile([P, CHANNELS], BF16)
        bias_sb = consts.tile([P, H, GROUPS], F32)

        make_identity(nc, ident[:])
        nc.vector.memset(ones[:], 1.0)
        nc.vector.memset(zeros[:], 0.0)
        nc.vector.memset(bias_rows[:], 0.0)
        nc.vector.memset(w_scales[:].bitcast(I32), 0)

        def load_tiles(n):
            first = sum(LOAD_TILES[:n])
            tiles = slice(first, first + LOAD_TILES[n])
            nc.sync.dma_start(out=x_sb[:, tiles, :], in_=x_rows[:, tiles, :])

        nc.sync.dma_start(out=bias_row[:], in_=b.rearrange("g h -> (g h)").unsqueeze(0))
        for n in range(W_BEHIND_LOADS):
            load_tiles(n)
        nc.sync.dma_start(
            out=w_codes[:].bitcast(I32),
            in_=W_words.rearrange("g p n t -> p g (n t)").bitcast(I32),
        )
        scale_rows = W_scales.rearrange("g (Q r) n -> r Q g n", r=4)
        for r in range(4):
            nc.sync.dma_start(out=w_scales[r:P:32, :, :].bitcast(I32), in_=scale_rows[r].bitcast(I32))
        for n in range(W_BEHIND_LOADS, len(LOAD_TILES)):
            load_tiles(n)

        def transpose_and_quantise(r):
            quantised = []
            for i in range(TILES_PER_ROUND):
                x_words = x_sb[:, r * TILES_PER_ROUND + i, :].bitcast(F32)
                grouped = stage.tile([P, GROUPS * P * PACK], BF16, align_bytes=64)
                grouped_words = grouped[:].bitcast(F32)
                for bank in range(GROUPS // BANK_GROUPS):
                    xt = xt_pool.tile([P, 2, BANK_GROUPS * P], F32, tag="xt")
                    for g2 in range(BANK_GROUPS):
                        first = (bank * BANK_GROUPS + g2) * WORDS_GROUP
                        for u in range(2):
                            nc.tensor.transpose(
                                xt[:, u, g2 * P : (g2 + 1) * P],
                                x_words[:, first + u : first + WORDS_GROUP : 2],
                                ident[:],
                            )
                    bank_words = slice(bank * 2 * BANK_GROUPS * P, (bank + 1) * 2 * BANK_GROUPS * P)
                    nc.scalar.copy(
                        out=grouped_words[:, bank_words].rearrange("p (c u) -> p c u", u=2),
                        in_=xt[:].rearrange("p u c -> p c u"),
                    )
                x_codes = stage.tile([P, GROUPS * P], U32, align_bytes=64)
                x_scales = stage.tile([P, GROUPS * P], U8, align_bytes=64)
                nc.vector.quantize_mx(out=x_codes[:].bitcast(FP8X4), scales=x_scales[:], in_=grouped[:])
                quantised.append((x_codes, x_scales))
            return quantised

        def multiply_and_store(r, quantised):
            for i in range(TILES_PER_ROUND):
                x_codes, x_scales = quantised[i]
                acc = acc_pool.tile([P, GROUPS, H], F32, tag="acc")
                for g in range(GROUPS):
                    tokens = slice(g * P, (g + 1) * P)
                    nc.tensor.matmul_mx(
                        out=acc[:, g, :],
                        lhsT=x_codes[:, tokens].bitcast(FP8X4),
                        lhsT_scale=x_scales[:, tokens],
                        rhs=w_codes[:, g, :].bitcast(FP8X4),
                        rhs_scale=w_scales[:, g, :],
                        start=True,
                        stop=True,
                    )
                nc.vector.tensor_tensor(
                    out=out_sb[:, r * TILES_PER_ROUND + i, :].rearrange("p (h g) -> p h g", g=GROUPS),
                    in0=acc[:].rearrange("p g h -> p h g"),
                    in1=bias_sb[:],
                    op=mybir.AluOpType.add,
                )
                done = r * TILES_PER_ROUND + i + 1
                for n in range(len(STORE_TILES)):
                    if sum(STORE_TILES[: n + 1]) == done:
                        tiles = slice(done - STORE_TILES[n], done)
                        nc.sync.dma_start(out=out_rows[:, tiles, :], in_=out_sb[:, tiles, :])

        def spread_bias():
            nc.vector.tensor_copy(out=bias_rows[0:1, :], in_=bias_row[:])
            bias_ps = acc_pool.tile([P, GROUPS, H], F32, tag="acc")
            nc.tensor.matmul(
                out=bias_ps[:].rearrange("p g h -> p (g h)"),
                lhsT=ones[:],
                rhs=bias_rows[:],
                start=True,
                stop=True,
            )
            nc.vector.tensor_copy(out=bias_sb[:], in_=bias_ps[:].rearrange("p g h -> p h g"))

        warm = xt_pool.tile([P, CHANNELS], F32, tag="xt")
        for n in range(WARM_UP):
            nc.tensor.matmul(out=warm[:], lhsT=ones[:], rhs=zeros[:], start=True, stop=True)
        spread_bias()
        waiting = transpose_and_quantise(0)
        for r in range(1, ROUNDS):
            fresh = transpose_and_quantise(r)
            multiply_and_store(r - 1, waiting)
            waiting = fresh
        multiply_and_store(ROUNDS - 1, waiting)
